import numpy as np
import ml_dtypes

BF16 = ml_dtypes.bfloat16


def bf(x):
    return np.asarray(x, np.float32).astype(BF16)


def f32(x):
    return np.asarray(x, np.float32)


def f64(x):
    return np.asarray(x).astype(np.float64)


def striped(idx):
    return np.tile(idx.reshape(-1, 16).T, (8, 1))


C, S, B, O, H, K, N = 256, 512, 2, 32, 256, 8, 2048


def setup_inputs():
    x = np.random.standard_normal((C, O))
    rel_t = np.random.standard_normal((C, S))
    w = np.random.standard_normal((C, C)) / np.sqrt(C)
    b = 0.1 * np.random.standard_normal((C, 1))
    idx = np.concatenate([np.random.permutation(S)[:H] for _ in range(K)])
    return {"rel_t": f32(rel_t), "xr": f32(np.tile(x, (1, B * O))), "w": bf(w), "b": f32(b), "offs": striped(idx)}


def reference(rel_t, xr, w, b, offs):
    idx = offs[:16].T.reshape(-1)
    prod = f64(rel_t)[:, idx] * f64(xr)
    return f64(w).T @ prod + f64(b)

@@ -1,0 +1,67 @@
+import concourse.mybir as mybir
+
+F32, BF16, U16 = mybir.dt.float32, mybir.dt.bfloat16, mybir.dt.uint16
+MULT = mybir.AluOpType.mult
+IDENTITY = mybir.ActivationFunctionType.Identity
+
+P = 128
+C = 256
+M = 256
+S = 512
+N = 2048
+C_BLOCKS = C // P
+M_BLOCKS = M // P
+PIECE = 512
+PIECES = N // PIECE
+OFFSET_COLUMNS = PIECE // 16
+
+FLOPS = 2 * C * M * N
+
+
+def tile_gcn_kernel(tc, rel_t, xr, w, b, offs, out):
+    nc = tc.nc
+    with (
+        tc.tile_pool(name="held", bufs=1) as held,
+        tc.tile_pool(name="work", bufs=4) as work,
+        tc.psum_pool(name="psum", bufs=2) as psum,
+    ):
+        offsets = held.tile([P, N // 16], U16, name="offsets")
+        nc.sync.dma_start(offsets[:], offs)
+
+        tables = [held.tile([P, S], F32, name=f"table{c}") for c in range(C_BLOCKS)]
+        weights = [held.tile([P, M], BF16, name=f"weights{c}") for c in range(C_BLOCKS)]
+        biases = [held.tile([P, 1], F32, name=f"bias{m}") for m in range(M_BLOCKS)]
+        for c in range(C_BLOCKS):
+            nc.scalar.dma_start(tables[c][:], rel_t[c * P : (c + 1) * P, :])
+        for c in range(C_BLOCKS):
+            nc.scalar.dma_start(weights[c][:], w[c * P : (c + 1) * P, :])
+        for m in range(M_BLOCKS):
+            nc.scalar.dma_start(biases[m][:], b[m * P : (m + 1) * P, :])
+
+        for j in range(PIECES):
+            columns = slice(j * PIECE, (j + 1) * PIECE)
+            piece_offsets = offsets[:, j * OFFSET_COLUMNS : (j + 1) * OFFSET_COLUMNS]
+
+            rounded = []
+            for c in range(C_BLOCKS):
+                objects = work.tile([P, PIECE], F32, name=f"objects{c}")
+                nc.sync.dma_start(objects[:], xr[c * P : (c + 1) * P, columns])
+                product = work.tile([P, PIECE], F32, name=f"product{c}")
+                nc.vector.tensor_tensor(product[:], tables[c][:].indirect(piece_offsets), objects[:], MULT)
+                product_bf = work.tile([P, PIECE], BF16, name=f"rounded{c}")
+                nc.scalar.copy(product_bf[:], product[:])
+                rounded.append(product_bf)
+
+            for m in range(M_BLOCKS):
+                bank = psum.tile([P, PIECE], F32, name=f"bank{m}")
+                for c in range(C_BLOCKS):
+                    nc.tensor.matmul(
+                        bank[:],
+                        weights[c][:, m * P : (m + 1) * P],
+                        rounded[c][:],
+                        start=(c == 0),
+                        stop=(c == C_BLOCKS - 1),
+                    )
+                message = work.tile([P, PIECE], F32, name=f"message{m}")
+                nc.scalar.activation(message[:], bank[:], IDENTITY, bias=biases[m][:])
+                nc.sync.dma_start(out[m * P : (m + 1) * P, columns], message[:])

@@ -1,7 +1,7 @@
 import concourse.mybir as mybir
 
 F32, BF16, U16 = mybir.dt.float32, mybir.dt.bfloat16, mybir.dt.uint16
-MULT = mybir.AluOpType.mult
+MULT, ADD = mybir.AluOpType.mult, mybir.AluOpType.add
 IDENTITY = mybir.ActivationFunctionType.Identity
 
 P = 128
@@ -11,9 +11,11 @@ S = 512
 N = 2048
 C_BLOCKS = C // P
 M_BLOCKS = M // P
-PIECE = 512
-PIECES = N // PIECE
-OFFSET_COLUMNS = PIECE // 16
+
+WIDTHS = (256, 512, 512, 256, 256, 256)
+assert sum(WIDTHS) == N
+STARTS = tuple(sum(WIDTHS[:j]) for j in range(len(WIDTHS)))
+PIECES = len(WIDTHS)
 
 FLOPS = 2 * C * M * N
 
@@ -22,46 +24,61 @@ def tile_gcn_kernel(tc, rel_t, xr, w, b, offs, out):
     nc = tc.nc
     with (
         tc.tile_pool(name="held", bufs=1) as held,
-        tc.tile_pool(name="work", bufs=4) as work,
         tc.psum_pool(name="psum", bufs=2) as psum,
     ):
         offsets = held.tile([P, N // 16], U16, name="offsets")
+        objects = [held.tile([P, N], F32, name=f"objects{c}") for c in range(C_BLOCKS)]
         nc.sync.dma_start(offsets[:], offs)
+        for j in range(PIECES):
+            columns = slice(STARTS[j], STARTS[j] + WIDTHS[j])
+            for c in range(C_BLOCKS):
+                nc.sync.dma_start(objects[c][:, columns], xr[c * P : (c + 1) * P, columns])
 
         tables = [held.tile([P, S], F32, name=f"table{c}") for c in range(C_BLOCKS)]
-        weights = [held.tile([P, M], BF16, name=f"weights{c}") for c in range(C_BLOCKS)]
-        biases = [held.tile([P, 1], F32, name=f"bias{m}") for m in range(M_BLOCKS)]
         for c in range(C_BLOCKS):
             nc.scalar.dma_start(tables[c][:], rel_t[c * P : (c + 1) * P, :])
-        for c in range(C_BLOCKS):
-            nc.scalar.dma_start(weights[c][:], w[c * P : (c + 1) * P, :])
-        for m in range(M_BLOCKS):
-            nc.scalar.dma_start(biases[m][:], b[m * P : (m + 1) * P, :])
+        weights = held.tile([P, C_BLOCKS, M], BF16, name="weights")
+        nc.scalar.dma_start(weights[:], w.rearrange("(c p) m -> p c m", p=P))
+        bias = held.tile([P, M_BLOCKS], F32, name="bias")
+        with nc.allow_non_contiguous_dma(reason="256 single values, one to a partition and block"):
+            nc.scalar.dma_start(bias[:], b.rearrange("(m p) o -> p (m o)", p=P))
 
+        products = [held.tile([P, N], F32, name=f"products{c}") for c in range(C_BLOCKS)]
+        rounded = [held.tile([P, N], BF16, name=f"rounded{c}") for c in range(C_BLOCKS)]
+        messages = [held.tile([P, N], F32, name=f"messages{m}") for m in range(M_BLOCKS)]
+
+        def evacuate(banks, j, m):
+            columns = slice(STARTS[j], STARTS[j] + WIDTHS[j])
+            if m == 1 and j >= PIECES - 2:
+                nc.vector.tensor_scalar(messages[m][:, columns], banks[m][:], bias[:, m : m + 1], None, ADD)
+                nc.scalar.dma_start(out[m * P : (m + 1) * P, columns], messages[m][:, columns])
+            else:
+                nc.scalar.activation(messages[m][:, columns], banks[m][:], IDENTITY, bias=bias[:, m : m + 1])
+                nc.sync.dma_start(out[m * P : (m + 1) * P, columns], messages[m][:, columns])
+
+        previous_banks = None
         for j in range(PIECES):
-            columns = slice(j * PIECE, (j + 1) * PIECE)
-            piece_offsets = offsets[:, j * OFFSET_COLUMNS : (j + 1) * OFFSET_COLUMNS]
-
-            rounded = []
+            columns = slice(STARTS[j], STARTS[j] + WIDTHS[j])
+            piece_offsets = offsets[:, STARTS[j] // 16 : (STARTS[j] + WIDTHS[j]) // 16]
+            banks = [psum.tile([P, WIDTHS[j]], F32, name=f"bank{m}") for m in range(M_BLOCKS)]
             for c in range(C_BLOCKS):
-                objects = work.tile([P, PIECE], F32, name=f"objects{c}")
-                nc.sync.dma_start(objects[:], xr[c * P : (c + 1) * P, columns])
-                product = work.tile([P, PIECE], F32, name=f"product{c}")
-                nc.vector.tensor_tensor(product[:], tables[c][:].indirect(piece_offsets), objects[:], MULT)
-                product_bf = work.tile([P, PIECE], BF16, name=f"rounded{c}")
-                nc.scalar.copy(product_bf[:], product[:])
-                rounded.append(product_bf)
-
-            for m in range(M_BLOCKS):
-                bank = psum.tile([P, PIECE], F32, name=f"bank{m}")
-                for c in range(C_BLOCKS):
+                nc.vector.tensor_tensor(
+                    products[c][:, columns], tables[c][:].indirect(piece_offsets), objects[c][:, columns], MULT
+                )
+                if (j, c) == (PIECES - 1, C_BLOCKS - 1):
+                    nc.vector.tensor_copy(rounded[c][:, columns], products[c][:, columns])
+                else:
+                    nc.scalar.copy(rounded[c][:, columns], products[c][:, columns])
+                for m in range(M_BLOCKS):
                     nc.tensor.matmul(
-                        bank[:],
-                        weights[c][:, m * P : (m + 1) * P],
-                        rounded[c][:],
+                        banks[m][:],
+                        weights[:, c, m * P : (m + 1) * P],
+                        rounded[c][:, columns],
                         start=(c == 0),
                         stop=(c == C_BLOCKS - 1),
                     )
-                message = work.tile([P, PIECE], F32, name=f"message{m}")
-                nc.scalar.activation(message[:], bank[:], IDENTITY, bias=biases[m][:])
-                nc.sync.dma_start(out[m * P : (m + 1) * P, columns], message[:])
+                if previous_banks is not None:
+                    evacuate(previous_banks, j - 1, c)
+            previous_banks = banks
+        for m in range(M_BLOCKS):
+            evacuate(previous_banks, PIECES - 1, m)

@@ -12,9 +12,11 @@ N = 2048
 C_BLOCKS = C // P
 M_BLOCKS = M // P
 
-WIDTHS = (256, 512, 512, 256, 256, 256)
+CHUNK = 512
+CHUNKS = N // CHUNK
+WIDTHS = (512, 512, 512, 256, 128, 128)
 assert sum(WIDTHS) == N
-STARTS = tuple(sum(WIDTHS[:j]) for j in range(len(WIDTHS)))
+STARTS = tuple(sum(WIDTHS[:p]) for p in range(len(WIDTHS)))
 PIECES = len(WIDTHS)
 
 FLOPS = 2 * C * M * N
@@ -24,13 +26,13 @@ def tile_gcn_kernel(tc, rel_t, xr, w, b, offs, out):
     nc = tc.nc
     with (
         tc.tile_pool(name="held", bufs=1) as held,
-        tc.psum_pool(name="psum", bufs=2) as psum,
+        tc.psum_pool(name="psum", bufs=4) as psum,
     ):
         offsets = held.tile([P, N // 16], U16, name="offsets")
         objects = [held.tile([P, N], F32, name=f"objects{c}") for c in range(C_BLOCKS)]
         nc.sync.dma_start(offsets[:], offs)
-        for j in range(PIECES):
-            columns = slice(STARTS[j], STARTS[j] + WIDTHS[j])
+        for k in range(CHUNKS):
+            columns = slice(k * CHUNK, (k + 1) * CHUNK)
             for c in range(C_BLOCKS):
                 nc.sync.dma_start(objects[c][:, columns], xr[c * P : (c + 1) * P, columns])
 
@@ -46,39 +48,56 @@ def tile_gcn_kernel(tc, rel_t, xr, w, b, offs, out):
         products = [held.tile([P, N], F32, name=f"products{c}") for c in range(C_BLOCKS)]
         rounded = [held.tile([P, N], BF16, name=f"rounded{c}") for c in range(C_BLOCKS)]
         messages = [held.tile([P, N], F32, name=f"messages{m}") for m in range(M_BLOCKS)]
+        banks = {}
 
-        def evacuate(banks, j, m):
-            columns = slice(STARTS[j], STARTS[j] + WIDTHS[j])
-            if m == 1 and j >= PIECES - 2:
-                nc.vector.tensor_scalar(messages[m][:, columns], banks[m][:], bias[:, m : m + 1], None, ADD)
+        def look_up(c, start, width, rounder):
+            columns = slice(start, start + width)
+            nc.vector.tensor_tensor(
+                products[c][:, columns],
+                tables[c][:].indirect(offsets[:, start // 16 : (start + width) // 16]),
+                objects[c][:, columns],
+                MULT,
+            )
+            if rounder == "vector":
+                nc.vector.tensor_copy(rounded[c][:, columns], products[c][:, columns])
+            else:
+                nc.scalar.copy(rounded[c][:, columns], products[c][:, columns])
+
+        def project(c, p):
+            columns = slice(STARTS[p], STARTS[p] + WIDTHS[p])
+            for m in range(M_BLOCKS):
+                if c == 0:
+                    banks[p, m] = psum.tile([P, WIDTHS[p]], F32, name=f"bank{m}")
+                nc.tensor.matmul(
+                    banks[p, m][:],
+                    weights[:, c, m * P : (m + 1) * P],
+                    rounded[c][:, columns],
+                    start=(c == 0),
+                    stop=(c == C_BLOCKS - 1),
+                )
+
+        def evacuate(p, m, engine):
+            columns = slice(STARTS[p], STARTS[p] + WIDTHS[p])
+            if engine == "vector":
+                nc.vector.tensor_scalar(messages[m][:, columns], banks[p, m][:], bias[:, m : m + 1], None, ADD)
                 nc.scalar.dma_start(out[m * P : (m + 1) * P, columns], messages[m][:, columns])
             else:
-                nc.scalar.activation(messages[m][:, columns], banks[m][:], IDENTITY, bias=bias[:, m : m + 1])
+                nc.scalar.activation(messages[m][:, columns], banks[p, m][:], IDENTITY, bias=bias[:, m : m + 1])
                 nc.sync.dma_start(out[m * P : (m + 1) * P, columns], messages[m][:, columns])
 
-        previous_banks = None
-        for j in range(PIECES):
-            columns = slice(STARTS[j], STARTS[j] + WIDTHS[j])
-            piece_offsets = offsets[:, STARTS[j] // 16 : (STARTS[j] + WIDTHS[j]) // 16]
-            banks = [psum.tile([P, WIDTHS[j]], F32, name=f"bank{m}") for m in range(M_BLOCKS)]
-            for c in range(C_BLOCKS):
-                nc.vector.tensor_tensor(
-                    products[c][:, columns], tables[c][:].indirect(piece_offsets), objects[c][:, columns], MULT
-                )
-                if (j, c) == (PIECES - 1, C_BLOCKS - 1):
-                    nc.vector.tensor_copy(rounded[c][:, columns], products[c][:, columns])
-                else:
-                    nc.scalar.copy(rounded[c][:, columns], products[c][:, columns])
-                for m in range(M_BLOCKS):
-                    nc.tensor.matmul(
-                        banks[m][:],
-                        weights[:, c, m * P : (m + 1) * P],
-                        rounded[c][:, columns],
-                        start=(c == 0),
-                        stop=(c == C_BLOCKS - 1),
-                    )
-                if previous_banks is not None:
-                    evacuate(previous_banks, j - 1, c)
-            previous_banks = banks
-        for m in range(M_BLOCKS):
-            evacuate(previous_banks, PIECES - 1, m)
+        due = []
+        for k in range(CHUNKS):
+            inside = [p for p in range(PIECES) if k * CHUNK <= STARTS[p] < (k + 1) * CHUNK]
+            look_up(0, k * CHUNK, CHUNK, "scalar")
+            for p in inside:
+                project(0, p)
+            if due:
+                evacuate(*due.pop(0), "scalar")
+            for p in inside:
+                look_up(1, STARTS[p], WIDTHS[p], "vector" if p == PIECES - 1 else "scalar")
+                project(1, p)
+                if due:
+                    evacuate(*due.pop(0), "scalar")
+                due.extend((p, m) for m in range(M_BLOCKS))
+        for p, m in due:
+            evacuate(p, m, "vector" if m == 1 else "scalar")

@@ -12,12 +12,13 @@ N = 2048
 C_BLOCKS = C // P
 M_BLOCKS = M // P
 
-CHUNK = 512
-CHUNKS = N // CHUNK
-WIDTHS = (512, 512, 512, 256, 128, 128)
-assert sum(WIDTHS) == N
+WIDTHS = (256, 512, 512, 256, 256, 256)
+CHUNK_WIDTHS = (256, 512, 512, 256, 512)
+assert sum(WIDTHS) == N and sum(CHUNK_WIDTHS) == N
 STARTS = tuple(sum(WIDTHS[:p]) for p in range(len(WIDTHS)))
+CHUNK_STARTS = tuple(sum(CHUNK_WIDTHS[:k]) for k in range(len(CHUNK_WIDTHS)))
 PIECES = len(WIDTHS)
+CHUNKS = len(CHUNK_WIDTHS)
 
 FLOPS = 2 * C * M * N
 
@@ -32,7 +33,7 @@ def tile_gcn_kernel(tc, rel_t, xr, w, b, offs, out):
         objects = [held.tile([P, N], F32, name=f"objects{c}") for c in range(C_BLOCKS)]
         nc.sync.dma_start(offsets[:], offs)
         for k in range(CHUNKS):
-            columns = slice(k * CHUNK, (k + 1) * CHUNK)
+            columns = slice(CHUNK_STARTS[k], CHUNK_STARTS[k] + CHUNK_WIDTHS[k])
             for c in range(C_BLOCKS):
                 nc.sync.dma_start(objects[c][:, columns], xr[c * P : (c + 1) * P, columns])
 
@@ -80,15 +81,15 @@ def tile_gcn_kernel(tc, rel_t, xr, w, b, offs, out):
             columns = slice(STARTS[p], STARTS[p] + WIDTHS[p])
             if engine == "vector":
                 nc.vector.tensor_scalar(messages[m][:, columns], banks[p, m][:], bias[:, m : m + 1], None, ADD)
-                nc.scalar.dma_start(out[m * P : (m + 1) * P, columns], messages[m][:, columns])
             else:
                 nc.scalar.activation(messages[m][:, columns], banks[p, m][:], IDENTITY, bias=bias[:, m : m + 1])
-                nc.sync.dma_start(out[m * P : (m + 1) * P, columns], messages[m][:, columns])
+            queue = nc.scalar if (p, m) == (PIECES - 1, 0) else nc.sync
+            queue.dma_start(out[m * P : (m + 1) * P, columns], messages[m][:, columns])
 
         due = []
         for k in range(CHUNKS):
-            inside = [p for p in range(PIECES) if k * CHUNK <= STARTS[p] < (k + 1) * CHUNK]
-            look_up(0, k * CHUNK, CHUNK, "scalar")
+            inside = [p for p in range(PIECES) if CHUNK_STARTS[k] <= STARTS[p] < CHUNK_STARTS[k] + CHUNK_WIDTHS[k]]
+            look_up(0, CHUNK_STARTS[k], CHUNK_WIDTHS[k], "scalar")
             for p in inside:
                 project(0, p)
             if due:
@@ -96,7 +97,7 @@ def tile_gcn_kernel(tc, rel_t, xr, w, b, offs, out):
             for p in inside:
                 look_up(1, STARTS[p], WIDTHS[p], "vector" if p == PIECES - 1 else "scalar")
                 project(1, p)
-                if due:
+                if due and k < CHUNKS - 1:
                     evacuate(*due.pop(0), "scalar")
                 due.extend((p, m) for m in range(M_BLOCKS))
         for p, m in due:

@@ -83,8 +83,7 @@ def tile_gcn_kernel(tc, rel_t, xr, w, b, offs, out):
                 nc.vector.tensor_scalar(messages[m][:, columns], banks[p, m][:], bias[:, m : m + 1], None, ADD)
             else:
                 nc.scalar.activation(messages[m][:, columns], banks[p, m][:], IDENTITY, bias=bias[:, m : m + 1])
-            queue = nc.scalar if (p, m) == (PIECES - 1, 0) else nc.sync
-            queue.dma_start(out[m * P : (m + 1) * P, columns], messages[m][:, columns])
+            nc.sync.dma_start(out[m * P : (m + 1) * P, columns], messages[m][:, columns])
 
         due = []
         for k in range(CHUNKS):

@@ -12,8 +12,8 @@ N = 2048
 C_BLOCKS = C // P
 M_BLOCKS = M // P
 
-WIDTHS = (256, 512, 512, 256, 256, 256)
-CHUNK_WIDTHS = (256, 512, 512, 256, 512)
+WIDTHS = (384, 512, 384, 256, 256, 256)
+CHUNK_WIDTHS = (384, 512, 384, 256, 512)
 assert sum(WIDTHS) == N and sum(CHUNK_WIDTHS) == N
 STARTS = tuple(sum(WIDTHS[:p]) for p in range(len(WIDTHS)))
 CHUNK_STARTS = tuple(sum(CHUNK_WIDTHS[:k]) for k in range(len(CHUNK_WIDTHS)))

@@ -32,19 +32,21 @@ def tile_gcn_kernel(tc, rel_t, xr, w, b, offs, out):
         offsets = held.tile([P, N // 16], U16, name="offsets")
         objects = [held.tile([P, N], F32, name=f"objects{c}") for c in range(C_BLOCKS)]
         nc.sync.dma_start(offsets[:], offs)
+        weights = held.tile([P, C_BLOCKS, M], BF16, name="weights")
+        bias = held.tile([P, M_BLOCKS], F32, name="bias")
         for k in range(CHUNKS):
             columns = slice(CHUNK_STARTS[k], CHUNK_STARTS[k] + CHUNK_WIDTHS[k])
             for c in range(C_BLOCKS):
                 nc.sync.dma_start(objects[c][:, columns], xr[c * P : (c + 1) * P, columns])
+                if (k, c) == (0, 1):
+                    nc.sync.dma_start(weights[:], w.rearrange("(c p) m -> p c m", p=P))
+                if (k, c) == (1, 0):
+                    with nc.allow_non_contiguous_dma(reason="256 single values, one to a partition and block"):
+                        nc.sync.dma_start(bias[:], b.rearrange("(m p) o -> p (m o)", p=P))
 
         tables = [held.tile([P, S], F32, name=f"table{c}") for c in range(C_BLOCKS)]
         for c in range(C_BLOCKS):
             nc.scalar.dma_start(tables[c][:], rel_t[c * P : (c + 1) * P, :])
-        weights = held.tile([P, C_BLOCKS, M], BF16, name="weights")
-        nc.scalar.dma_start(weights[:], w.rearrange("(c p) m -> p c m", p=P))
-        bias = held.tile([P, M_BLOCKS], F32, name="bias")
-        with nc.allow_non_contiguous_dma(reason="256 single values, one to a partition and block"):
-            nc.scalar.dma_start(bias[:], b.rearrange("(m p) o -> p (m o)", p=P))
 
         products = [held.tile([P, N], F32, name=f"products{c}") for c in range(C_BLOCKS)]
         rounded = [held.tile([P, N], BF16, name=f"rounded{c}") for c in range(C_BLOCKS)]

@@ -53,7 +53,7 @@ def tile_gcn_kernel(tc, rel_t, xr, w, b, offs, out):
         messages = [held.tile([P, N], F32, name=f"messages{m}") for m in range(M_BLOCKS)]
         banks = {}
 
-        def look_up(c, start, width, rounder):
+        def look_up(c, start, width):
             columns = slice(start, start + width)
             nc.vector.tensor_tensor(
                 products[c][:, columns],
@@ -61,6 +61,9 @@ def tile_gcn_kernel(tc, rel_t, xr, w, b, offs, out):
                 objects[c][:, columns],
                 MULT,
             )
+
+        def round_product(c, p, rounder):
+            columns = slice(STARTS[p], STARTS[p] + WIDTHS[p])
             if rounder == "vector":
                 nc.vector.tensor_copy(rounded[c][:, columns], products[c][:, columns])
             else:
@@ -90,16 +93,18 @@ def tile_gcn_kernel(tc, rel_t, xr, w, b, offs, out):
         due = []
         for k in range(CHUNKS):
             inside = [p for p in range(PIECES) if CHUNK_STARTS[k] <= STARTS[p] < CHUNK_STARTS[k] + CHUNK_WIDTHS[k]]
-            look_up(0, CHUNK_STARTS[k], CHUNK_WIDTHS[k], "scalar")
+            look_up(0, CHUNK_STARTS[k], CHUNK_WIDTHS[k])
             for p in inside:
+                round_product(0, p, "scalar")
                 project(0, p)
-            if due:
+            if due and k < CHUNKS - 1:
                 evacuate(*due.pop(0), "scalar")
             for p in inside:
-                look_up(1, STARTS[p], WIDTHS[p], "vector" if p == PIECES - 1 else "scalar")
+                look_up(1, STARTS[p], WIDTHS[p])
+                round_product(1, p, "vector" if p == PIECES - 1 else "scalar")
                 project(1, p)
                 if due and k < CHUNKS - 1:
                     evacuate(*due.pop(0), "scalar")
                 due.extend((p, m) for m in range(M_BLOCKS))
         for p, m in due:
-            evacuate(p, m, "vector" if m == 1 else "scalar")
+            evacuate(p, m, "vector" if m == 1 and p in inside else "scalar")

@@ -12,13 +12,10 @@ N = 2048
 C_BLOCKS = C // P
 M_BLOCKS = M // P
 
-WIDTHS = (384, 512, 384, 256, 256, 256)
-CHUNK_WIDTHS = (384, 512, 384, 256, 512)
-assert sum(WIDTHS) == N and sum(CHUNK_WIDTHS) == N
+WIDTHS = (384, 512, 512, 384, 256)
+assert sum(WIDTHS) == N
 STARTS = tuple(sum(WIDTHS[:p]) for p in range(len(WIDTHS)))
-CHUNK_STARTS = tuple(sum(CHUNK_WIDTHS[:k]) for k in range(len(CHUNK_WIDTHS)))
 PIECES = len(WIDTHS)
-CHUNKS = len(CHUNK_WIDTHS)
 
 FLOPS = 2 * C * M * N
 
@@ -34,13 +31,13 @@ def tile_gcn_kernel(tc, rel_t, xr, w, b, offs, out):
         nc.sync.dma_start(offsets[:], offs)
         weights = held.tile([P, C_BLOCKS, M], BF16, name="weights")
         bias = held.tile([P, M_BLOCKS], F32, name="bias")
-        for k in range(CHUNKS):
-            columns = slice(CHUNK_STARTS[k], CHUNK_STARTS[k] + CHUNK_WIDTHS[k])
+        for p in range(PIECES):
+            columns = slice(STARTS[p], STARTS[p] + WIDTHS[p])
             for c in range(C_BLOCKS):
                 nc.sync.dma_start(objects[c][:, columns], xr[c * P : (c + 1) * P, columns])
-                if (k, c) == (0, 1):
+                if (p, c) == (0, 1):
                     nc.sync.dma_start(weights[:], w.rearrange("(c p) m -> p c m", p=P))
-                if (k, c) == (1, 0):
+                if (p, c) == (1, 0):
                     with nc.allow_non_contiguous_dma(reason="256 single values, one to a partition and block"):
                         nc.sync.dma_start(bias[:], b.rearrange("(m p) o -> p (m o)", p=P))
 
@@ -53,7 +50,8 @@ def tile_gcn_kernel(tc, rel_t, xr, w, b, offs, out):
         messages = [held.tile([P, N], F32, name=f"messages{m}") for m in range(M_BLOCKS)]
         banks = {}
 
-        def look_up(c, start, width):
+        def look_up(c, p):
+            start, width = STARTS[p], WIDTHS[p]
             columns = slice(start, start + width)
             nc.vector.tensor_tensor(
                 products[c][:, columns],
@@ -91,20 +89,25 @@ def tile_gcn_kernel(tc, rel_t, xr, w, b, offs, out):
             nc.sync.dma_start(out[m * P : (m + 1) * P, columns], messages[m][:, columns])
 
         due = []
-        for k in range(CHUNKS):
-            inside = [p for p in range(PIECES) if CHUNK_STARTS[k] <= STARTS[p] < CHUNK_STARTS[k] + CHUNK_WIDTHS[k]]
-            look_up(0, CHUNK_STARTS[k], CHUNK_WIDTHS[k])
-            for p in inside:
-                round_product(0, p, "scalar")
-                project(0, p)
-            if due and k < CHUNKS - 1:
+        for p in range(PIECES):
+            last = p == PIECES - 1
+            look_up(0, p)
+            if last:
+                round_product(1, p - 1, "vector")
+                project(1, p - 1)
+            round_product(0, p, "scalar")
+            project(0, p)
+            if due and not last:
                 evacuate(*due.pop(0), "scalar")
-            for p in inside:
-                look_up(1, STARTS[p], WIDTHS[p])
-                round_product(1, p, "vector" if p == PIECES - 1 else "scalar")
+            look_up(1, p)
+            if p < PIECES - 2:
+                round_product(1, p, "scalar")
                 project(1, p)
-                if due and k < CHUNKS - 1:
-                    evacuate(*due.pop(0), "scalar")
-                due.extend((p, m) for m in range(M_BLOCKS))
+            if last:
+                round_product(1, p, "vector")
+                project(1, p)
+            if due and not last:
+                evacuate(*due.pop(0), "scalar")
+            due.extend((p, m) for m in range(M_BLOCKS))
         for p, m in due:
-            evacuate(p, m, "vector" if m == 1 and p in inside else "scalar")
+            evacuate(p, m, "vector" if (p, m) == (PIECES - 1, M_BLOCKS - 1) else "scalar")

@@ -12,10 +12,11 @@ N = 2048
 C_BLOCKS = C // P
 M_BLOCKS = M // P
 
-WIDTHS = (384, 512, 512, 384, 256)
+WIDTHS = (384, 512, 384, 384, 256, 128)
 assert sum(WIDTHS) == N
 STARTS = tuple(sum(WIDTHS[:p]) for p in range(len(WIDTHS)))
 PIECES = len(WIDTHS)
+BY_VECTOR = PIECES - 2
 
 FLOPS = 2 * C * M * N
 
@@ -27,19 +28,25 @@ def tile_gcn_kernel(tc, rel_t, xr, w, b, offs, out):
         tc.psum_pool(name="psum", bufs=4) as psum,
     ):
         offsets = held.tile([P, N // 16], U16, name="offsets")
-        objects = [held.tile([P, N], F32, name=f"objects{c}") for c in range(C_BLOCKS)]
+        objects = held.tile([P, C_BLOCKS, N], F32, name="objects")
         nc.sync.dma_start(offsets[:], offs)
         weights = held.tile([P, C_BLOCKS, M], BF16, name="weights")
         bias = held.tile([P, M_BLOCKS], F32, name="bias")
-        for p in range(PIECES):
+        by_block = xr.rearrange("(c p) n -> p c n", p=P)
+
+        def load_block(c, p):
             columns = slice(STARTS[p], STARTS[p] + WIDTHS[p])
-            for c in range(C_BLOCKS):
-                nc.sync.dma_start(objects[c][:, columns], xr[c * P : (c + 1) * P, columns])
-                if (p, c) == (0, 1):
-                    nc.sync.dma_start(weights[:], w.rearrange("(c p) m -> p c m", p=P))
-                if (p, c) == (1, 0):
-                    with nc.allow_non_contiguous_dma(reason="256 single values, one to a partition and block"):
-                        nc.sync.dma_start(bias[:], b.rearrange("(m p) o -> p (m o)", p=P))
+            nc.sync.dma_start(objects[:, c, columns], by_block[:, c, columns])
+
+        load_block(0, 0)
+        load_block(1, 0)
+        nc.sync.dma_start(weights[:], w.rearrange("(c p) m -> p c m", p=P))
+        load_block(0, 1)
+        with nc.allow_non_contiguous_dma(reason="256 single values, one to a partition and block"):
+            nc.sync.dma_start(bias[:], b.rearrange("(m p) o -> p (m o)", p=P))
+        load_block(1, 1)
+        for start, stop in ((STARTS[2], STARTS[3]), (STARTS[3], STARTS[4]), (STARTS[4], N)):
+            nc.sync.dma_start(objects[:, :, start:stop], by_block[:, :, start:stop])
 
         tables = [held.tile([P, S], F32, name=f"table{c}") for c in range(C_BLOCKS)]
         for c in range(C_BLOCKS):
@@ -56,7 +63,7 @@ def tile_gcn_kernel(tc, rel_t, xr, w, b, offs, out):
             nc.vector.tensor_tensor(
                 products[c][:, columns],
                 tables[c][:].indirect(offsets[:, start // 16 : (start + width) // 16]),
-                objects[c][:, columns],
+                objects[:, c, columns],
                 MULT,
             )
 
@@ -88,26 +95,21 @@ def tile_gcn_kernel(tc, rel_t, xr, w, b, offs, out):
                 nc.scalar.activation(messages[m][:, columns], banks[p, m][:], IDENTITY, bias=bias[:, m : m + 1])
             nc.sync.dma_start(out[m * P : (m + 1) * P, columns], messages[m][:, columns])
 
-        due = []
+        due, held_back = [], []
         for p in range(PIECES):
-            last = p == PIECES - 1
-            look_up(0, p)
-            if last:
-                round_product(1, p - 1, "vector")
-                project(1, p - 1)
-            round_product(0, p, "scalar")
-            project(0, p)
-            if due and not last:
-                evacuate(*due.pop(0), "scalar")
-            look_up(1, p)
-            if p < PIECES - 2:
-                round_product(1, p, "scalar")
-                project(1, p)
-            if last:
-                round_product(1, p, "vector")
-                project(1, p)
-            if due and not last:
-                evacuate(*due.pop(0), "scalar")
+            for c in range(C_BLOCKS):
+                look_up(c, p)
+                if p < BY_VECTOR:
+                    round_product(c, p, "scalar")
+                    project(c, p)
+                    if due and p < BY_VECTOR - 1:
+                        evacuate(*due.pop(0), "scalar")
+                else:
+                    held_back.append((c, p))
+                    for product in held_back if (c, p) == (C_BLOCKS - 1, PIECES - 1) else held_back[:-1]:
+                        round_product(*product, "vector")
+                        project(*product)
+                    held_back = held_back[-1:]
             due.extend((p, m) for m in range(M_BLOCKS))
         for p, m in due:
             evacuate(p, m, "vector" if (p, m) == (PIECES - 1, M_BLOCKS - 1) else "scalar")

@@ -112,4 +112,4 @@ def tile_gcn_kernel(tc, rel_t, xr, w, b, offs, out):
                     held_back = held_back[-1:]
             due.extend((p, m) for m in range(M_BLOCKS))
         for p, m in due:
-            evacuate(p, m, "vector" if (p, m) == (PIECES - 1, M_BLOCKS - 1) else "scalar")
+            evacuate(p, m, "vector" if m == 1 and p >= BY_VECTOR else "scalar")

@@ -12,7 +12,7 @@ N = 2048
 C_BLOCKS = C // P
 M_BLOCKS = M // P
 
-WIDTHS = (384, 512, 384, 384, 256, 128)
+WIDTHS = (384, 512, 448, 320, 256, 128)
 assert sum(WIDTHS) == N
 STARTS = tuple(sum(WIDTHS[:p]) for p in range(len(WIDTHS)))
 PIECES = len(WIDTHS)

import concourse.mybir as mybir

F32, BF16, U16 = mybir.dt.float32, mybir.dt.bfloat16, mybir.dt.uint16
MULT, ADD = mybir.AluOpType.mult, mybir.AluOpType.add
IDENTITY = mybir.ActivationFunctionType.Identity

P = 128
C = 256
M = 256
S = 512
N = 2048
C_BLOCKS = C // P
M_BLOCKS = M // P

WIDTHS = (384, 512, 448, 320, 256, 128)
assert sum(WIDTHS) == N
STARTS = tuple(sum(WIDTHS[:p]) for p in range(len(WIDTHS)))
PIECES = len(WIDTHS)
BY_VECTOR = PIECES - 2

FLOPS = 2 * C * M * N


def tile_gcn_kernel(tc, rel_t, xr, w, b, offs, out):
    nc = tc.nc
    with (
        tc.tile_pool(name="held", bufs=1) as held,
        tc.psum_pool(name="psum", bufs=4) as psum,
    ):
        offsets = held.tile([P, N // 16], U16, name="offsets")
        objects = held.tile([P, C_BLOCKS, N], F32, name="objects")
        nc.sync.dma_start(offsets[:], offs)
        weights = held.tile([P, C_BLOCKS, M], BF16, name="weights")
        bias = held.tile([P, M_BLOCKS], F32, name="bias")
        by_block = xr.rearrange("(c p) n -> p c n", p=P)

        def load_block(c, p):
            columns = slice(STARTS[p], STARTS[p] + WIDTHS[p])
            nc.sync.dma_start(objects[:, c, columns], by_block[:, c, columns])

        load_block(0, 0)
        load_block(1, 0)
        nc.sync.dma_start(weights[:], w.rearrange("(c p) m -> p c m", p=P))
        load_block(0, 1)
        with nc.allow_non_contiguous_dma(reason="256 single values, one to a partition and block"):
            nc.sync.dma_start(bias[:], b.rearrange("(m p) o -> p (m o)", p=P))
        load_block(1, 1)
        for start, stop in ((STARTS[2], STARTS[3]), (STARTS[3], STARTS[4]), (STARTS[4], N)):
            nc.sync.dma_start(objects[:, :, start:stop], by_block[:, :, start:stop])

        tables = [held.tile([P, S], F32, name=f"table{c}") for c in range(C_BLOCKS)]
        for c in range(C_BLOCKS):
            nc.scalar.dma_start(tables[c][:], rel_t[c * P : (c + 1) * P, :])

        products = [held.tile([P, N], F32, name=f"products{c}") for c in range(C_BLOCKS)]
        rounded = [held.tile([P, N], BF16, name=f"rounded{c}") for c in range(C_BLOCKS)]
        messages = [held.tile([P, N], F32, name=f"messages{m}") for m in range(M_BLOCKS)]
        banks = {}

        def look_up(c, p):
            start, width = STARTS[p], WIDTHS[p]
            columns = slice(start, start + width)
            nc.vector.tensor_tensor(
                products[c][:, columns],
                tables[c][:].indirect(offsets[:, start // 16 : (start + width) // 16]),
                objects[:, c, columns],
                MULT,
            )

        def round_product(c, p, rounder):
            columns = slice(STARTS[p], STARTS[p] + WIDTHS[p])
            if rounder == "vector":
                nc.vector.tensor_copy(rounded[c][:, columns], products[c][:, columns])
            else:
                nc.scalar.copy(rounded[c][:, columns], products[c][:, columns])

        def project(c, p):
            columns = slice(STARTS[p], STARTS[p] + WIDTHS[p])
            for m in range(M_BLOCKS):
                if c == 0:
                    banks[p, m] = psum.tile([P, WIDTHS[p]], F32, name=f"bank{m}")
                nc.tensor.matmul(
                    banks[p, m][:],
                    weights[:, c, m * P : (m + 1) * P],
                    rounded[c][:, columns],
                    start=(c == 0),
                    stop=(c == C_BLOCKS - 1),
                )

        def evacuate(p, m, engine):
            columns = slice(STARTS[p], STARTS[p] + WIDTHS[p])
            if engine == "vector":
                nc.vector.tensor_scalar(messages[m][:, columns], banks[p, m][:], bias[:, m : m + 1], None, ADD)
            else:
                nc.scalar.activation(messages[m][:, columns], banks[p, m][:], IDENTITY, bias=bias[:, m : m + 1])
            nc.sync.dma_start(out[m * P : (m + 1) * P, columns], messages[m][:, columns])

        due, held_back = [], []
        for p in range(PIECES):
            for c in range(C_BLOCKS):
                look_up(c, p)
                if p < BY_VECTOR:
                    round_product(c, p, "scalar")
                    project(c, p)
                    if due and p < BY_VECTOR - 1:
                        evacuate(*due.pop(0), "scalar")
                else:
                    held_back.append((c, p))
                    for product in held_back if (c, p) == (C_BLOCKS - 1, PIECES - 1) else held_back[:-1]:
                        round_product(*product, "vector")
                        project(*product)
                    held_back = held_back[-1:]
            due.extend((p, m) for m in range(M_BLOCKS))
        for p, m in due:
            evacuate(p, m, "vector" if m == 1 and p >= BY_VECTOR else "scalar")
